import numpy as np
import ml_dtypes


def mxq(x, axis, fmt="e4m3"):
    dtype, down = {"e4m3": (ml_dtypes.float8_e4m3fn, 7), "e5m2": (ml_dtypes.float8_e5m2, 14)}[fmt]
    v = np.moveaxis(np.asarray(x, np.float32).astype(ml_dtypes.bfloat16).astype(np.float64), axis, -1)
    blocks = v.reshape(v.shape[:-1] + (-1, 32))
    amax = np.abs(blocks).max(-1, keepdims=True)
    byte = np.maximum(np.where(amax > 0, np.frexp(amax)[1] - 1 + 127, 0) - down, 1)
    scale = np.exp2(byte - 127.0)
    codes = (blocks / scale).astype(np.float32).astype(dtype).astype(np.float64)
    return np.moveaxis((codes * scale).reshape(v.shape), -1, axis)


WIDE = False


def mx_kscale(k):
    if not WIDE:
        return np.ones(k)
    levels = np.array([10, -10, 5, -5, 0])
    a = np.random.permutation(np.resize(levels, k // 512 * 4)).reshape(k // 512, 4)
    idx = np.arange(k)
    return np.exp2(a[idx // 512, idx % 128 // 32])


BF16 = ml_dtypes.bfloat16


def bf(x):
    return np.asarray(x, np.float32).astype(BF16)


def f64(x):
    return np.asarray(x).astype(np.float64)


B, K, H, D = 128, 128, 512, 64
C = 0.2
HALF_LOG_2PI = 0.5 * np.log(2.0 * np.pi)


def log_softmax(v, axis):
    v = v - v.max(axis=axis, keepdims=True)
    return v - np.log(np.exp(v).sum(axis=axis, keepdims=True))


def logsumexp(v, axis):
    m = v.max(axis=axis, keepdims=True)
    return np.log(np.exp(v - m).sum(axis=axis)) + np.squeeze(m, axis)


def contract(xq, vq):
    return (xq.transpose(2, 0, 1) @ vq.transpose(2, 1, 0)).transpose(1, 2, 0)


def setup_inputs():
    s = mx_kscale(H)[None, :, None]
    r = 1.0 / np.sqrt(H)
    return {
        "x": bf(np.random.standard_normal((B, H, D)) * s),
        "input_var": bf(np.random.standard_normal((B, D)) * C),
        "V_alpha": bf(np.random.standard_normal((K, H, D)) * r / s),
        "V_mu": bf(np.random.standard_normal((K, H, D)) * C * r / s),
        "V_sigma": bf(np.random.standard_normal((K, H, D)) * 0.5 * r / s),
        "b_alpha": bf(np.random.standard_normal((K, D)) * 0.7),
        "b_mu": bf(np.random.standard_normal((K, D)) * 0.5 * C),
        "b_sigma": bf(np.log(C) + np.random.standard_normal((K, D)) * 0.3),
    }


def reference(x, input_var, V_alpha, V_mu, V_sigma, b_alpha, b_mu, b_sigma):
    xq = mxq(f64(x), 1, "e4m3")
    exp_alpha = contract(xq, mxq(f64(V_alpha), 1, "e4m3")) + f64(b_alpha)
    log_alpha = log_softmax(exp_alpha, 1)
    mu = contract(xq, mxq(f64(V_mu), 1, "e4m3")) + f64(b_mu)
    log_sigma = np.clip(contract(xq, mxq(f64(V_sigma), 1, "e4m3")) + f64(b_sigma), -20.0, 20.0)
    sigma = np.exp(log_sigma)
    y = f64(input_var)[:, None, :]
    log_p = -0.5 * np.square((y - mu) / sigma) + log_alpha - HALF_LOG_2PI - log_sigma
    return np.sum(logsumexp(log_p, 1), axis=1)

@@ -1,0 +1,241 @@
+import math
+
+import concourse.mybir as mybir
+from concourse.masks import make_identity
+
+BF16 = mybir.dt.bfloat16
+F32 = mybir.dt.float32
+U32 = mybir.dt.uint32
+U8 = mybir.dt.uint8
+FP8X4 = mybir.dt.float8_e4m3fn_x4
+ALU = mybir.AluOpType
+ACT = mybir.ActivationFunctionType
+AX = mybir.AxisListType
+
+P = 128
+ROWS = 128
+H = 512
+D = 64
+PACK = 4
+HALF = 64
+CHUNK = 8
+RUN = 4
+D_VECTOR = 32
+GROUP = 4
+N_GROUPS = D // GROUP
+HALF_LOG_2PI = 0.5 * math.log(2.0 * math.pi)
+
+FLOPS = 2 * ROWS * ROWS * H * D * 3
+
+
+def load_and_quantise(nc, raw_pool, grouped_pool, src, codes, scales):
+    by_partition = src.rearrange("r (p j) d -> p r (j d)", j=PACK)
+    for half in range(ROWS // HALF):
+        grouped = grouped_pool.tile([P, D, HALF * PACK], BF16, align_bytes=64)
+        for c in range(HALF // CHUNK):
+            first_row = half * HALF + c * CHUNK
+            raw = raw_pool.tile([P, CHUNK, PACK * D], BF16)
+            nc.sync.dma_start(out=raw[:], in_=by_partition[:, first_row : first_row + CHUNK, :])
+            raw_mj = raw[:].rearrange("p r (j d) -> p (r j) d", j=PACK)
+            cols = slice(c * CHUNK * PACK, (c + 1) * CHUNK * PACK)
+            for copy, d_range in (
+                (nc.vector.tensor_copy, slice(0, D_VECTOR)),
+                (nc.scalar.copy, slice(D_VECTOR, D)),
+            ):
+                copy(
+                    out=grouped[:, d_range, cols].rearrange("p (c i) m -> p c m i", i=RUN),
+                    in_=raw_mj[:, :, d_range].rearrange("p m (c i) -> p c m i", i=RUN),
+                )
+        rows = slice(half * HALF, (half + 1) * HALF)
+        for d in range(D):
+            nc.vector.quantize_mx(
+                out=codes[:, d, rows].bitcast(FP8X4),
+                scales=scales[:, d, rows],
+                in_=grouped[:, d, :],
+            )
+
+
+def products(nc, psum, w_codes, w_scales, x_codes, x_scales, group):
+    acc = psum.tile([P, GROUP, ROWS], F32, tag="acc")
+    for i in range(GROUP):
+        d = group * GROUP + i
+        nc.tensor.matmul_mx(
+            out=acc[:, i, :],
+            lhsT=w_codes[:, d, :].bitcast(FP8X4),
+            lhsT_scale=w_scales[:, d, :],
+            rhs=x_codes[:, d, :].bitcast(FP8X4),
+            rhs_scale=x_scales[:, d, :],
+            start=True,
+            stop=True,
+        )
+    return acc
+
+
+def tile_rnadeoutputlayer_kernel(
+    tc, x, input_var, V_alpha, V_mu, V_sigma, b_alpha, b_mu, b_sigma, out
+):
+    nc = tc.nc
+    with (
+        tc.tile_pool(name="keep", bufs=1) as keep,
+        tc.tile_pool(name="raw", bufs=4) as raw_pool,
+        tc.tile_pool(name="grouped", bufs=2) as grouped_pool,
+        tc.psum_pool(name="acc", bufs=4) as psum_acc,
+        tc.psum_pool(name="tp", bufs=4) as psum_tp,
+    ):
+        ident = keep.tile([P, P], F32)
+        make_identity(nc, ident[:])
+
+        bias_bf = keep.tile([P, 3, D], BF16)
+        nc.scalar.dma_start(out=bias_bf[:, 0, :], in_=b_sigma)
+        nc.scalar.dma_start(out=bias_bf[:, 1, :], in_=b_mu)
+        nc.scalar.dma_start(out=bias_bf[:, 2, :], in_=b_alpha)
+        bias_sigma = keep.tile([P, D], F32)
+        bias_mu = keep.tile([P, D], F32)
+        neg_bias_alpha = keep.tile([P, D], F32)
+        nc.vector.tensor_copy(out=bias_sigma[:], in_=bias_bf[:, 0, :])
+        nc.vector.tensor_copy(out=bias_mu[:], in_=bias_bf[:, 1, :])
+        nc.vector.tensor_scalar(
+            out=neg_bias_alpha[:], in0=bias_bf[:, 2, :], scalar1=-1.0, scalar2=None, op0=ALU.mult
+        )
+
+        x_codes = keep.tile([P, D, ROWS], U32, align_bytes=64)
+        x_scales = keep.tile([P, D, ROWS], U8, align_bytes=64)
+        w_codes = keep.tile([P, D, ROWS], U32, align_bytes=64)
+        w_scales = keep.tile([P, D, ROWS], U8, align_bytes=64)
+
+        load_and_quantise(nc, raw_pool, grouped_pool, x, x_codes, x_scales)
+
+        y_all = keep.tile([P, D, ROWS], BF16)
+        with tc.tile_pool(name="setup", bufs=1) as setup:
+            y_rows = setup.tile([P, ROWS, D], BF16)
+            nc.sync.dma_start(
+                out=y_rows[:].rearrange("p b d -> p (b d)"),
+                in_=input_var.rearrange("b d -> (b d)").partition_broadcast(P),
+            )
+            nc.scalar.copy(
+                out=y_all[:].rearrange("p (c i) b -> p c b i", i=RUN),
+                in_=y_rows[:].rearrange("p b (c i) -> p c b i", i=RUN),
+            )
+
+        with (
+            tc.tile_pool(name="late", bufs=1) as late,
+            tc.tile_pool(name="work", bufs=2) as work,
+        ):
+            load_and_quantise(nc, raw_pool, grouped_pool, V_sigma, w_codes, w_scales)
+            penalty = late.tile([P, D, ROWS], F32)
+            for g in range(N_GROUPS):
+                ds = slice(g * GROUP, (g + 1) * GROUP)
+                acc = products(nc, psum_acc, w_codes, w_scales, x_codes, x_scales, g)
+                for i in range(GROUP):
+                    d = g * GROUP + i
+                    nc.scalar.activation(
+                        out=penalty[:, d, :],
+                        in_=acc[:, i, :],
+                        func=ACT.Identity,
+                        bias=bias_sigma[:, d : d + 1],
+                        scale=1.0,
+                    )
+                nc.vector.tensor_scalar(
+                    out=penalty[:, ds, :],
+                    in0=penalty[:, ds, :],
+                    scalar1=-20.0,
+                    scalar2=20.0,
+                    op0=ALU.max,
+                    op1=ALU.min,
+                )
+
+            load_and_quantise(nc, raw_pool, grouped_pool, V_mu, w_codes, w_scales)
+            for g in range(N_GROUPS):
+                ds = slice(g * GROUP, (g + 1) * GROUP)
+                acc = products(nc, psum_acc, w_codes, w_scales, x_codes, x_scales, g)
+                inv_sigma = work.tile([P, GROUP, ROWS], F32, tag="first")
+                nc.scalar.activation(
+                    out=inv_sigma[:], in_=penalty[:, ds, :], func=ACT.Exp, scale=-1.0
+                )
+                z = work.tile([P, GROUP, ROWS], F32, tag="second")
+                for i in range(GROUP):
+                    d = g * GROUP + i
+                    nc.vector.scalar_tensor_tensor(
+                        out=z[:, i, :],
+                        in0=acc[:, i, :],
+                        scalar=bias_mu[:, d : d + 1],
+                        in1=y_all[:, d, :],
+                        op0=ALU.add,
+                        op1=ALU.subtract,
+                    )
+                nc.vector.tensor_tensor(out=z[:], in0=z[:], in1=inv_sigma[:], op=ALU.mult)
+                nc.scalar.activation(out=z[:], in_=z[:], func=ACT.Square, scale=math.sqrt(0.5))
+                nc.vector.tensor_tensor(
+                    out=penalty[:, ds, :], in0=penalty[:, ds, :], in1=z[:], op=ALU.add
+                )
+
+            load_and_quantise(nc, raw_pool, grouped_pool, V_alpha, w_codes, w_scales)
+            neg_max = late.tile([P, 2, D], F32)
+            exp_sum = late.tile([P, 2, D], F32)
+            for g in range(N_GROUPS):
+                ds = slice(g * GROUP, (g + 1) * GROUP)
+                acc = products(nc, psum_acc, w_codes, w_scales, x_codes, x_scales, g)
+                neg_a = work.tile([P, GROUP, ROWS], F32, tag="first")
+                for i in range(GROUP):
+                    d = g * GROUP + i
+                    nc.scalar.activation(
+                        out=neg_a[:, i, :],
+                        in_=acc[:, i, :],
+                        func=ACT.Identity,
+                        bias=neg_bias_alpha[:, d : d + 1],
+                        scale=-1.0,
+                    )
+                neg_lp = work.tile([P, GROUP, ROWS], F32, tag="second")
+                nc.vector.tensor_tensor(
+                    out=neg_lp[:], in0=neg_a[:], in1=penalty[:, ds, :], op=ALU.add
+                )
+                for w, source in enumerate((neg_a, neg_lp)):
+                    by_b = psum_tp.tile([P, GROUP, ROWS], F32, tag="tp")
+                    for i in range(GROUP):
+                        nc.tensor.transpose(by_b[:, i, :], source[:, i, :], ident[:])
+                    nc.vector.tensor_reduce(
+                        out=neg_max[:, w, ds], in_=by_b[:], axis=AX.X, op=ALU.min
+                    )
+                    unused = work.tile([P, GROUP, ROWS], F32, tag="third")
+                    for i in range(GROUP):
+                        d = g * GROUP + i
+                        nc.scalar.activation(
+                            out=unused[:, i, :],
+                            in_=by_b[:, i, :],
+                            func=ACT.Exp,
+                            bias=neg_max[:, w, d : d + 1],
+                            scale=-1.0,
+                            accum_out=exp_sum[:, w, d : d + 1],
+                        )
+
+            log_sum = late.tile([P, 2, D], F32)
+            log_total = late.tile([P, 2], F32)
+            for w in range(2):
+                nc.scalar.activation(
+                    out=log_sum[:, w, :],
+                    in_=exp_sum[:, w, :],
+                    func=ACT.Ln,
+                    accum_out=log_total[:, w : w + 1],
+                )
+            neg_max_total = late.tile([P, 2], F32)
+            nc.vector.tensor_reduce(out=neg_max_total[:], in_=neg_max[:], axis=AX.X, op=ALU.add)
+            lse_total = late.tile([P, 2], F32)
+            nc.vector.tensor_tensor(
+                out=lse_total[:], in0=log_total[:], in1=neg_max_total[:], op=ALU.subtract
+            )
+            result = late.tile([P, 1], F32)
+            nc.vector.tensor_scalar(
+                out=result[:],
+                in0=lse_total[:, 1:2],
+                scalar1=lse_total[:, 0:1],
+                scalar2=-D * HALF_LOG_2PI,
+                op0=ALU.subtract,
+                op1=ALU.add,
+            )
+            repeated = late.tile([P, P], F32)
+            nc.vector.tensor_copy(out=repeated[:], in_=result[:].to_broadcast([P, P]))
+            as_row = psum_tp.tile([P, P], F32, tag="tp")
+            nc.tensor.transpose(as_row[:], repeated[:], ident[:])
+            row = late.tile([P, P], F32)
+            nc.vector.tensor_copy(out=row[:], in_=as_row[:])
+            nc.sync.dma_start(out=out.rearrange("(o b) -> o b", o=1), in_=row[0:1, :])

@@ -20,7 +20,7 @@ PACK = 4
 HALF = 64
 CHUNK = 8
 RUN = 4
-D_VECTOR = 32
+D_VECTOR = 40
 GROUP = 4
 N_GROUPS = D // GROUP
 HALF_LOG_2PI = 0.5 * math.log(2.0 * math.pi)
@@ -77,7 +77,7 @@ def tile_rnadeoutputlayer_kernel(
     nc = tc.nc
     with (
         tc.tile_pool(name="keep", bufs=1) as keep,
-        tc.tile_pool(name="raw", bufs=4) as raw_pool,
+        tc.tile_pool(name="raw", bufs=7) as raw_pool,
         tc.tile_pool(name="grouped", bufs=2) as grouped_pool,
         tc.psum_pool(name="acc", bufs=4) as psum_acc,
         tc.psum_pool(name="tp", bufs=4) as psum_tp,
@@ -185,18 +185,31 @@ def tile_rnadeoutputlayer_kernel(
                         bias=neg_bias_alpha[:, d : d + 1],
                         scale=-1.0,
                     )
-                neg_lp = work.tile([P, GROUP, ROWS], F32, tag="second")
-                nc.vector.tensor_tensor(
-                    out=neg_lp[:], in0=neg_a[:], in1=penalty[:, ds, :], op=ALU.add
-                )
-                for w, source in enumerate((neg_a, neg_lp)):
+                for w in range(2):
                     by_b = psum_tp.tile([P, GROUP, ROWS], F32, tag="tp")
                     for i in range(GROUP):
-                        nc.tensor.transpose(by_b[:, i, :], source[:, i, :], ident[:])
+                        d = g * GROUP + i
+                        nc.tensor.matmul(
+                            out=by_b[:, i, :],
+                            lhsT=neg_a[:, i, :],
+                            rhs=ident[:],
+                            is_transpose=True,
+                            start=True,
+                            stop=(w == 0),
+                        )
+                        if w == 1:
+                            nc.tensor.matmul(
+                                out=by_b[:, i, :],
+                                lhsT=penalty[:, d, :],
+                                rhs=ident[:],
+                                is_transpose=True,
+                                start=False,
+                                stop=True,
+                            )
                     nc.vector.tensor_reduce(
                         out=neg_max[:, w, ds], in_=by_b[:], axis=AX.X, op=ALU.min
                     )
-                    unused = work.tile([P, GROUP, ROWS], F32, tag="third")
+                    unused = work.tile([P, GROUP, ROWS], F32, tag="second")
                     for i in range(GROUP):
                         d = g * GROUP + i
                         nc.scalar.activation(

@@ -20,18 +20,18 @@ PACK = 4
 HALF = 64
 CHUNK = 8
 RUN = 4
-D_VECTOR = 40
+D_SCALAR = 24
 GROUP = 4
 N_GROUPS = D // GROUP
+GROUPS_PER_CHUNK = N_GROUPS // (HALF // CHUNK)
 HALF_LOG_2PI = 0.5 * math.log(2.0 * math.pi)
 
 FLOPS = 2 * ROWS * ROWS * H * D * 3
 
 
-def load_and_quantise(nc, raw_pool, grouped_pool, src, codes, scales):
+def load_and_quantise(nc, raw_pool, grouped, src, codes, scales, older_work=None):
     by_partition = src.rearrange("r (p j) d -> p r (j d)", j=PACK)
     for half in range(ROWS // HALF):
-        grouped = grouped_pool.tile([P, D, HALF * PACK], BF16, align_bytes=64)
         for c in range(HALF // CHUNK):
             first_row = half * HALF + c * CHUNK
             raw = raw_pool.tile([P, CHUNK, PACK * D], BF16)
@@ -39,13 +39,16 @@ def load_and_quantise(nc, raw_pool, grouped_pool, src, codes, scales):
             raw_mj = raw[:].rearrange("p r (j d) -> p (r j) d", j=PACK)
             cols = slice(c * CHUNK * PACK, (c + 1) * CHUNK * PACK)
             for copy, d_range in (
-                (nc.vector.tensor_copy, slice(0, D_VECTOR)),
-                (nc.scalar.copy, slice(D_VECTOR, D)),
+                (nc.scalar.copy, slice(0, D_SCALAR)),
+                (nc.vector.tensor_copy, slice(D_SCALAR, D)),
             ):
                 copy(
                     out=grouped[:, d_range, cols].rearrange("p (c i) m -> p c m i", i=RUN),
                     in_=raw_mj[:, :, d_range].rearrange("p m (c i) -> p c m i", i=RUN),
                 )
+            if older_work is not None and half == 0:
+                for g in range(c * GROUPS_PER_CHUNK, (c + 1) * GROUPS_PER_CHUNK):
+                    older_work(g)
         rows = slice(half * HALF, (half + 1) * HALF)
         for d in range(D):
             nc.vector.quantize_mx(
@@ -55,22 +58,6 @@ def load_and_quantise(nc, raw_pool, grouped_pool, src, codes, scales):
             )
 
 
-def products(nc, psum, w_codes, w_scales, x_codes, x_scales, group):
-    acc = psum.tile([P, GROUP, ROWS], F32, tag="acc")
-    for i in range(GROUP):
-        d = group * GROUP + i
-        nc.tensor.matmul_mx(
-            out=acc[:, i, :],
-            lhsT=w_codes[:, d, :].bitcast(FP8X4),
-            lhsT_scale=w_scales[:, d, :],
-            rhs=x_codes[:, d, :].bitcast(FP8X4),
-            rhs_scale=x_scales[:, d, :],
-            start=True,
-            stop=True,
-        )
-    return acc
-
-
 def tile_rnadeoutputlayer_kernel(
     tc, x, input_var, V_alpha, V_mu, V_sigma, b_alpha, b_mu, b_sigma, out
 ):
@@ -78,7 +65,7 @@ def tile_rnadeoutputlayer_kernel(
     with (
         tc.tile_pool(name="keep", bufs=1) as keep,
         tc.tile_pool(name="raw", bufs=7) as raw_pool,
-        tc.tile_pool(name="grouped", bufs=2) as grouped_pool,
+        tc.tile_pool(name="work", bufs=2) as work,
         tc.psum_pool(name="acc", bufs=4) as psum_acc,
         tc.psum_pool(name="tp", bufs=4) as psum_tp,
     ):
@@ -98,14 +85,74 @@ def tile_rnadeoutputlayer_kernel(
             out=neg_bias_alpha[:], in0=bias_bf[:, 2, :], scalar1=-1.0, scalar2=None, op0=ALU.mult
         )
 
+        grouped = keep.tile([P, D, HALF * PACK], BF16, align_bytes=64)
         x_codes = keep.tile([P, D, ROWS], U32, align_bytes=64)
         x_scales = keep.tile([P, D, ROWS], U8, align_bytes=64)
         w_codes = keep.tile([P, D, ROWS], U32, align_bytes=64)
         w_scales = keep.tile([P, D, ROWS], U8, align_bytes=64)
-
-        load_and_quantise(nc, raw_pool, grouped_pool, x, x_codes, x_scales)
-
+        neg_a = keep.tile([P, D, ROWS], F32)
         y_all = keep.tile([P, D, ROWS], BF16)
+        neg_max = keep.tile([P, 2, D], F32)
+        exp_sum = keep.tile([P, 2, D], F32)
+
+        def products(g):
+            acc = psum_acc.tile([P, GROUP, ROWS], F32, tag="acc")
+            for i in range(GROUP):
+                d = g * GROUP + i
+                nc.tensor.matmul_mx(
+                    out=acc[:, i, :],
+                    lhsT=w_codes[:, d, :].bitcast(FP8X4),
+                    lhsT_scale=w_scales[:, d, :],
+                    rhs=x_codes[:, d, :].bitcast(FP8X4),
+                    rhs_scale=x_scales[:, d, :],
+                    start=True,
+                    stop=True,
+                )
+            return acc
+
+        def reduce_over_k(g, w, terms_of):
+            by_b = psum_tp.tile([P, GROUP, ROWS], F32, tag="tp")
+            for i in range(GROUP):
+                terms = terms_of(i)
+                for t, term in enumerate(terms):
+                    nc.tensor.matmul(
+                        out=by_b[:, i, :],
+                        lhsT=term,
+                        rhs=ident[:],
+                        is_transpose=True,
+                        start=(t == 0),
+                        stop=(t == len(terms) - 1),
+                    )
+            ds = slice(g * GROUP, (g + 1) * GROUP)
+            nc.vector.tensor_reduce(out=neg_max[:, w, ds], in_=by_b[:], axis=AX.X, op=ALU.min)
+            unused = work.tile([P, GROUP, ROWS], F32, tag="unused")
+            for i in range(GROUP):
+                d = g * GROUP + i
+                nc.scalar.activation(
+                    out=unused[:, i, :],
+                    in_=by_b[:, i, :],
+                    func=ACT.Exp,
+                    bias=neg_max[:, w, d : d + 1],
+                    scale=-1.0,
+                    accum_out=exp_sum[:, w, d : d + 1],
+                )
+
+        def alpha_group(g):
+            acc = products(g)
+            for i in range(GROUP):
+                d = g * GROUP + i
+                nc.scalar.activation(
+                    out=neg_a[:, d, :],
+                    in_=acc[:, i, :],
+                    func=ACT.Identity,
+                    bias=neg_bias_alpha[:, d : d + 1],
+                    scale=-1.0,
+                )
+            reduce_over_k(g, 0, lambda i: [neg_a[:, g * GROUP + i, :]])
+
+        load_and_quantise(nc, raw_pool, grouped, x, x_codes, x_scales)
+        load_and_quantise(nc, raw_pool, grouped, V_alpha, w_codes, w_scales)
+
         with tc.tile_pool(name="setup", bufs=1) as setup:
             y_rows = setup.tile([P, ROWS, D], BF16)
             nc.sync.dma_start(
@@ -117,109 +164,68 @@ def tile_rnadeoutputlayer_kernel(
                 in_=y_rows[:].rearrange("p b (c i) -> p c b i", i=RUN),
             )
 
-        with (
-            tc.tile_pool(name="late", bufs=1) as late,
-            tc.tile_pool(name="work", bufs=2) as work,
-        ):
-            load_and_quantise(nc, raw_pool, grouped_pool, V_sigma, w_codes, w_scales)
-            penalty = late.tile([P, D, ROWS], F32)
-            for g in range(N_GROUPS):
+        with tc.tile_pool(name="late", bufs=1) as late:
+            log_sigma = late.tile([P, D, ROWS], F32)
+
+            def sigma_group(g):
                 ds = slice(g * GROUP, (g + 1) * GROUP)
-                acc = products(nc, psum_acc, w_codes, w_scales, x_codes, x_scales, g)
+                acc = products(g)
                 for i in range(GROUP):
                     d = g * GROUP + i
                     nc.scalar.activation(
-                        out=penalty[:, d, :],
+                        out=log_sigma[:, d, :],
                         in_=acc[:, i, :],
                         func=ACT.Identity,
                         bias=bias_sigma[:, d : d + 1],
                         scale=1.0,
                     )
                 nc.vector.tensor_scalar(
-                    out=penalty[:, ds, :],
-                    in0=penalty[:, ds, :],
+                    out=log_sigma[:, ds, :],
+                    in0=log_sigma[:, ds, :],
                     scalar1=-20.0,
                     scalar2=20.0,
                     op0=ALU.max,
                     op1=ALU.min,
                 )
 
-            load_and_quantise(nc, raw_pool, grouped_pool, V_mu, w_codes, w_scales)
-            for g in range(N_GROUPS):
+            def mu_group(g):
                 ds = slice(g * GROUP, (g + 1) * GROUP)
-                acc = products(nc, psum_acc, w_codes, w_scales, x_codes, x_scales, g)
-                inv_sigma = work.tile([P, GROUP, ROWS], F32, tag="first")
+                acc = products(g)
+                inv_sigma = work.tile([P, GROUP, ROWS], F32, tag="inv_sigma")
                 nc.scalar.activation(
-                    out=inv_sigma[:], in_=penalty[:, ds, :], func=ACT.Exp, scale=-1.0
+                    out=inv_sigma[:], in_=log_sigma[:, ds, :], func=ACT.Exp, scale=-1.0
                 )
-                z = work.tile([P, GROUP, ROWS], F32, tag="second")
+                half_z2 = work.tile([P, GROUP, ROWS], F32, tag="half_z2")
                 for i in range(GROUP):
                     d = g * GROUP + i
                     nc.vector.scalar_tensor_tensor(
-                        out=z[:, i, :],
+                        out=half_z2[:, i, :],
                         in0=acc[:, i, :],
                         scalar=bias_mu[:, d : d + 1],
                         in1=y_all[:, d, :],
                         op0=ALU.add,
                         op1=ALU.subtract,
                     )
-                nc.vector.tensor_tensor(out=z[:], in0=z[:], in1=inv_sigma[:], op=ALU.mult)
-                nc.scalar.activation(out=z[:], in_=z[:], func=ACT.Square, scale=math.sqrt(0.5))
                 nc.vector.tensor_tensor(
-                    out=penalty[:, ds, :], in0=penalty[:, ds, :], in1=z[:], op=ALU.add
+                    out=half_z2[:], in0=half_z2[:], in1=inv_sigma[:], op=ALU.mult
+                )
+                nc.scalar.activation(
+                    out=half_z2[:], in_=half_z2[:], func=ACT.Square, scale=math.sqrt(0.5)
+                )
+                reduce_over_k(
+                    g,
+                    1,
+                    lambda i: [
+                        neg_a[:, g * GROUP + i, :],
+                        log_sigma[:, g * GROUP + i, :],
+                        half_z2[:, i, :],
+                    ],
                 )
 
-            load_and_quantise(nc, raw_pool, grouped_pool, V_alpha, w_codes, w_scales)
-            neg_max = late.tile([P, 2, D], F32)
-            exp_sum = late.tile([P, 2, D], F32)
+            load_and_quantise(nc, raw_pool, grouped, V_sigma, w_codes, w_scales, alpha_group)
+            load_and_quantise(nc, raw_pool, grouped, V_mu, w_codes, w_scales, sigma_group)
             for g in range(N_GROUPS):
-                ds = slice(g * GROUP, (g + 1) * GROUP)
-                acc = products(nc, psum_acc, w_codes, w_scales, x_codes, x_scales, g)
-                neg_a = work.tile([P, GROUP, ROWS], F32, tag="first")
-                for i in range(GROUP):
-                    d = g * GROUP + i
-                    nc.scalar.activation(
-                        out=neg_a[:, i, :],
-                        in_=acc[:, i, :],
-                        func=ACT.Identity,
-                        bias=neg_bias_alpha[:, d : d + 1],
-                        scale=-1.0,
-                    )
-                for w in range(2):
-                    by_b = psum_tp.tile([P, GROUP, ROWS], F32, tag="tp")
-                    for i in range(GROUP):
-                        d = g * GROUP + i
-                        nc.tensor.matmul(
-                            out=by_b[:, i, :],
-                            lhsT=neg_a[:, i, :],
-                            rhs=ident[:],
-                            is_transpose=True,
-                            start=True,
-                            stop=(w == 0),
-                        )
-                        if w == 1:
-                            nc.tensor.matmul(
-                                out=by_b[:, i, :],
-                                lhsT=penalty[:, d, :],
-                                rhs=ident[:],
-                                is_transpose=True,
-                                start=False,
-                                stop=True,
-                            )
-                    nc.vector.tensor_reduce(
-                        out=neg_max[:, w, ds], in_=by_b[:], axis=AX.X, op=ALU.min
-                    )
-                    unused = work.tile([P, GROUP, ROWS], F32, tag="second")
-                    for i in range(GROUP):
-                        d = g * GROUP + i
-                        nc.scalar.activation(
-                            out=unused[:, i, :],
-                            in_=by_b[:, i, :],
-                            func=ACT.Exp,
-                            bias=neg_max[:, w, d : d + 1],
-                            scale=-1.0,
-                            accum_out=exp_sum[:, w, d : d + 1],
-                        )
+                mu_group(g)
 
             log_sum = late.tile([P, 2, D], F32)
             log_total = late.tile([P, 2], F32)

@@ -23,13 +23,12 @@ RUN = 4
 D_SCALAR = 24
 GROUP = 4
 N_GROUPS = D // GROUP
-GROUPS_PER_CHUNK = N_GROUPS // (HALF // CHUNK)
 HALF_LOG_2PI = 0.5 * math.log(2.0 * math.pi)
 
 FLOPS = 2 * ROWS * ROWS * H * D * 3
 
 
-def load_and_quantise(nc, raw_pool, grouped, src, codes, scales, older_work=None):
+def load_and_quantise(nc, raw_pool, grouped, src, codes, scales, other_work=None):
     by_partition = src.rearrange("r (p j) d -> p r (j d)", j=PACK)
     for half in range(ROWS // HALF):
         for c in range(HALF // CHUNK):
@@ -46,9 +45,8 @@ def load_and_quantise(nc, raw_pool, grouped, src, codes, scales, older_work=None
                     out=grouped[:, d_range, cols].rearrange("p (c i) m -> p c m i", i=RUN),
                     in_=raw_mj[:, :, d_range].rearrange("p m (c i) -> p c m i", i=RUN),
                 )
-            if older_work is not None and half == 0:
-                for g in range(c * GROUPS_PER_CHUNK, (c + 1) * GROUPS_PER_CHUNK):
-                    older_work(g)
+            if other_work is not None:
+                other_work(first_row // CHUNK)
         rows = slice(half * HALF, (half + 1) * HALF)
         for d in range(D):
             nc.vector.quantize_mx(
@@ -71,7 +69,11 @@ def tile_rnadeoutputlayer_kernel(
     ):
         ident = keep.tile([P, P], F32)
         make_identity(nc, ident[:])
+        ident_bf = keep.tile([P, P], BF16)
+        make_identity(nc, ident_bf[:])
 
+        y_bf = keep.tile([P, D], BF16)
+        nc.scalar.dma_start(out=y_bf[:], in_=input_var)
         bias_bf = keep.tile([P, 3, D], BF16)
         nc.scalar.dma_start(out=bias_bf[:, 0, :], in_=b_sigma)
         nc.scalar.dma_start(out=bias_bf[:, 1, :], in_=b_mu)
@@ -125,7 +127,7 @@ def tile_rnadeoutputlayer_kernel(
                     )
             ds = slice(g * GROUP, (g + 1) * GROUP)
             nc.vector.tensor_reduce(out=neg_max[:, w, ds], in_=by_b[:], axis=AX.X, op=ALU.min)
-            unused = work.tile([P, GROUP, ROWS], F32, tag="unused")
+            unused = work.tile([P, GROUP, ROWS], BF16, tag="unused")
             for i in range(GROUP):
                 d = g * GROUP + i
                 nc.scalar.activation(
@@ -137,56 +139,49 @@ def tile_rnadeoutputlayer_kernel(
                     accum_out=exp_sum[:, w, d : d + 1],
                 )
 
-        def alpha_group(g):
-            acc = products(g)
+        for g in range(N_GROUPS):
+            spread = psum_acc.tile([P, GROUP, ROWS], F32, tag="acc")
             for i in range(GROUP):
                 d = g * GROUP + i
-                nc.scalar.activation(
-                    out=neg_a[:, d, :],
-                    in_=acc[:, i, :],
-                    func=ACT.Identity,
-                    bias=neg_bias_alpha[:, d : d + 1],
-                    scale=-1.0,
+                nc.tensor.matmul(
+                    out=spread[:, i, :],
+                    lhsT=y_bf[:, d : d + 1].to_broadcast([P, P]),
+                    rhs=ident_bf[:],
+                    start=True,
+                    stop=True,
                 )
-            reduce_over_k(g, 0, lambda i: [neg_a[:, g * GROUP + i, :]])
+            nc.scalar.copy(out=y_all[:, g * GROUP : (g + 1) * GROUP, :], in_=spread[:])
 
         load_and_quantise(nc, raw_pool, grouped, x, x_codes, x_scales)
         load_and_quantise(nc, raw_pool, grouped, V_alpha, w_codes, w_scales)
 
-        with tc.tile_pool(name="setup", bufs=1) as setup:
-            y_rows = setup.tile([P, ROWS, D], BF16)
-            nc.sync.dma_start(
-                out=y_rows[:].rearrange("p b d -> p (b d)"),
-                in_=input_var.rearrange("b d -> (b d)").partition_broadcast(P),
-            )
-            nc.scalar.copy(
-                out=y_all[:].rearrange("p (c i) b -> p c b i", i=RUN),
-                in_=y_rows[:].rearrange("p b (c i) -> p c b i", i=RUN),
-            )
+        for g in range(N_GROUPS):
+            acc = products(g)
+            for i in range(GROUP):
+                d = g * GROUP + i
+                if g % 2 == 0:
+                    nc.scalar.activation(
+                        out=neg_a[:, d, :],
+                        in_=acc[:, i, :],
+                        func=ACT.Identity,
+                        bias=neg_bias_alpha[:, d : d + 1],
+                        scale=-1.0,
+                    )
+                else:
+                    nc.vector.tensor_scalar(
+                        out=neg_a[:, d, :],
+                        in0=acc[:, i, :],
+                        scalar1=-1.0,
+                        scalar2=neg_bias_alpha[:, d : d + 1],
+                        op0=ALU.mult,
+                        op1=ALU.add,
+                    )
+
+        def alpha_group(g):
+            reduce_over_k(g, 0, lambda i: [neg_a[:, g * GROUP + i, :]])
 
         with tc.tile_pool(name="late", bufs=1) as late:
             log_sigma = late.tile([P, D, ROWS], F32)
-
-            def sigma_group(g):
-                ds = slice(g * GROUP, (g + 1) * GROUP)
-                acc = products(g)
-                for i in range(GROUP):
-                    d = g * GROUP + i
-                    nc.scalar.activation(
-                        out=log_sigma[:, d, :],
-                        in_=acc[:, i, :],
-                        func=ACT.Identity,
-                        bias=bias_sigma[:, d : d + 1],
-                        scale=1.0,
-                    )
-                nc.vector.tensor_scalar(
-                    out=log_sigma[:, ds, :],
-                    in0=log_sigma[:, ds, :],
-                    scalar1=-20.0,
-                    scalar2=20.0,
-                    op0=ALU.max,
-                    op1=ALU.min,
-                )
 
             def mu_group(g):
                 ds = slice(g * GROUP, (g + 1) * GROUP)
@@ -195,7 +190,7 @@ def tile_rnadeoutputlayer_kernel(
                 nc.scalar.activation(
                     out=inv_sigma[:], in_=log_sigma[:, ds, :], func=ACT.Exp, scale=-1.0
                 )
-                half_z2 = work.tile([P, GROUP, ROWS], F32, tag="half_z2")
+                half_z2 = work.tile([P, GROUP, ROWS], F32, tag="half_z2", bufs=3)
                 for i in range(GROUP):
                     d = g * GROUP + i
                     nc.vector.scalar_tensor_tensor(
@@ -223,7 +218,29 @@ def tile_rnadeoutputlayer_kernel(
                 )
 
             load_and_quantise(nc, raw_pool, grouped, V_sigma, w_codes, w_scales, alpha_group)
-            load_and_quantise(nc, raw_pool, grouped, V_mu, w_codes, w_scales, sigma_group)
+
+            for g in range(N_GROUPS):
+                ds = slice(g * GROUP, (g + 1) * GROUP)
+                acc = products(g)
+                for i in range(GROUP):
+                    d = g * GROUP + i
+                    nc.scalar.activation(
+                        out=log_sigma[:, d, :],
+                        in_=acc[:, i, :],
+                        func=ACT.Identity,
+                        bias=bias_sigma[:, d : d + 1],
+                        scale=1.0,
+                    )
+                nc.vector.tensor_scalar(
+                    out=log_sigma[:, ds, :],
+                    in0=log_sigma[:, ds, :],
+                    scalar1=-20.0,
+                    scalar2=20.0,
+                    op0=ALU.max,
+                    op1=ALU.min,
+                )
+
+            load_and_quantise(nc, raw_pool, grouped, V_mu, w_codes, w_scales)
             for g in range(N_GROUPS):
                 mu_group(g)
 

@@ -20,17 +20,19 @@ PACK = 4
 HALF = 64
 CHUNK = 8
 RUN = 4
-D_SCALAR = 24
+D_VECTOR = 40
 GROUP = 4
 N_GROUPS = D // GROUP
 HALF_LOG_2PI = 0.5 * math.log(2.0 * math.pi)
+CLIP = 20.0
 
 FLOPS = 2 * ROWS * ROWS * H * D * 3
 
 
-def load_and_quantise(nc, raw_pool, grouped, src, codes, scales, other_work=None):
+def load_and_quantise(nc, raw_pool, grouped_tiles, src, codes, scales, other_work=None):
     by_partition = src.rearrange("r (p j) d -> p r (j d)", j=PACK)
     for half in range(ROWS // HALF):
+        grouped = grouped_tiles[half % len(grouped_tiles)]
         for c in range(HALF // CHUNK):
             first_row = half * HALF + c * CHUNK
             raw = raw_pool.tile([P, CHUNK, PACK * D], BF16)
@@ -38,8 +40,8 @@ def load_and_quantise(nc, raw_pool, grouped, src, codes, scales, other_work=None
             raw_mj = raw[:].rearrange("p r (j d) -> p (r j) d", j=PACK)
             cols = slice(c * CHUNK * PACK, (c + 1) * CHUNK * PACK)
             for copy, d_range in (
-                (nc.scalar.copy, slice(0, D_SCALAR)),
-                (nc.vector.tensor_copy, slice(D_SCALAR, D)),
+                (nc.vector.tensor_copy, slice(0, D_VECTOR)),
+                (nc.scalar.copy, slice(D_VECTOR, D)),
             ):
                 copy(
                     out=grouped[:, d_range, cols].rearrange("p (c i) m -> p c m i", i=RUN),
@@ -78,10 +80,12 @@ def tile_rnadeoutputlayer_kernel(
         nc.scalar.dma_start(out=bias_bf[:, 0, :], in_=b_sigma)
         nc.scalar.dma_start(out=bias_bf[:, 1, :], in_=b_mu)
         nc.scalar.dma_start(out=bias_bf[:, 2, :], in_=b_alpha)
-        bias_sigma = keep.tile([P, D], F32)
+        bias_sigma_up = keep.tile([P, D], F32)
         bias_mu = keep.tile([P, D], F32)
         neg_bias_alpha = keep.tile([P, D], F32)
-        nc.vector.tensor_copy(out=bias_sigma[:], in_=bias_bf[:, 0, :])
+        nc.vector.tensor_scalar(
+            out=bias_sigma_up[:], in0=bias_bf[:, 0, :], scalar1=CLIP, scalar2=None, op0=ALU.add
+        )
         nc.vector.tensor_copy(out=bias_mu[:], in_=bias_bf[:, 1, :])
         nc.vector.tensor_scalar(
             out=neg_bias_alpha[:], in0=bias_bf[:, 2, :], scalar1=-1.0, scalar2=None, op0=ALU.mult
@@ -94,6 +98,8 @@ def tile_rnadeoutputlayer_kernel(
         w_scales = keep.tile([P, D, ROWS], U8, align_bytes=64)
         neg_a = keep.tile([P, D, ROWS], F32)
         y_all = keep.tile([P, D, ROWS], BF16)
+        clip_bias = keep.tile([P, 1], F32)
+        nc.vector.memset(clip_bias[:], CLIP)
         neg_max = keep.tile([P, 2, D], F32)
         exp_sum = keep.tile([P, 2, D], F32)
 
@@ -152,43 +158,53 @@ def tile_rnadeoutputlayer_kernel(
                 )
             nc.scalar.copy(out=y_all[:, g * GROUP : (g + 1) * GROUP, :], in_=spread[:])
 
-        load_and_quantise(nc, raw_pool, grouped, x, x_codes, x_scales)
-        load_and_quantise(nc, raw_pool, grouped, V_alpha, w_codes, w_scales)
+        with tc.tile_pool(name="early", bufs=1) as early:
+            grouped_too = early.tile([P, D, HALF * PACK], BF16, align_bytes=64)
+            two_grouped = [grouped, grouped_too]
 
-        for g in range(N_GROUPS):
-            acc = products(g)
-            for i in range(GROUP):
-                d = g * GROUP + i
-                if g % 2 == 0:
-                    nc.scalar.activation(
-                        out=neg_a[:, d, :],
-                        in_=acc[:, i, :],
-                        func=ACT.Identity,
-                        bias=neg_bias_alpha[:, d : d + 1],
-                        scale=-1.0,
-                    )
-                else:
-                    nc.vector.tensor_scalar(
-                        out=neg_a[:, d, :],
-                        in0=acc[:, i, :],
-                        scalar1=-1.0,
-                        scalar2=neg_bias_alpha[:, d : d + 1],
-                        op0=ALU.mult,
-                        op1=ALU.add,
-                    )
+            load_and_quantise(nc, raw_pool, two_grouped, x, x_codes, x_scales)
+            load_and_quantise(nc, raw_pool, two_grouped, V_alpha, w_codes, w_scales)
 
-        def alpha_group(g):
-            reduce_over_k(g, 0, lambda i: [neg_a[:, g * GROUP + i, :]])
+            for g in range(N_GROUPS):
+                acc = products(g)
+                for i in range(GROUP):
+                    d = g * GROUP + i
+                    if g % 2 == 0:
+                        nc.scalar.activation(
+                            out=neg_a[:, d, :],
+                            in_=acc[:, i, :],
+                            func=ACT.Identity,
+                            bias=neg_bias_alpha[:, d : d + 1],
+                            scale=-1.0,
+                        )
+                    else:
+                        nc.vector.tensor_scalar(
+                            out=neg_a[:, d, :],
+                            in0=acc[:, i, :],
+                            scalar1=-1.0,
+                            scalar2=neg_bias_alpha[:, d : d + 1],
+                            op0=ALU.mult,
+                            op1=ALU.add,
+                        )
+
+            def alpha_group(g):
+                reduce_over_k(g, 0, lambda i: [neg_a[:, g * GROUP + i, :]])
+
+            load_and_quantise(nc, raw_pool, two_grouped, V_sigma, w_codes, w_scales, alpha_group)
 
         with tc.tile_pool(name="late", bufs=1) as late:
-            log_sigma = late.tile([P, D, ROWS], F32)
+            sigma_up = late.tile([P, D, ROWS], F32)
 
             def mu_group(g):
                 ds = slice(g * GROUP, (g + 1) * GROUP)
                 acc = products(g)
                 inv_sigma = work.tile([P, GROUP, ROWS], F32, tag="inv_sigma")
                 nc.scalar.activation(
-                    out=inv_sigma[:], in_=log_sigma[:, ds, :], func=ACT.Exp, scale=-1.0
+                    out=inv_sigma[:],
+                    in_=sigma_up[:, ds, :],
+                    func=ACT.Exp,
+                    bias=clip_bias[:],
+                    scale=-1.0,
                 )
                 half_z2 = work.tile([P, GROUP, ROWS], F32, tag="half_z2", bufs=3)
                 for i in range(GROUP):
@@ -201,8 +217,13 @@ def tile_rnadeoutputlayer_kernel(
                         op0=ALU.add,
                         op1=ALU.subtract,
                     )
-                nc.vector.tensor_tensor(
-                    out=half_z2[:], in0=half_z2[:], in1=inv_sigma[:], op=ALU.mult
+                nc.vector.scalar_tensor_tensor(
+                    out=half_z2[:],
+                    in0=inv_sigma[:],
+                    scalar=math.exp(-CLIP),
+                    in1=half_z2[:],
+                    op0=ALU.max,
+                    op1=ALU.mult,
                 )
                 nc.scalar.activation(
                     out=half_z2[:], in_=half_z2[:], func=ACT.Square, scale=math.sqrt(0.5)
@@ -210,14 +231,8 @@ def tile_rnadeoutputlayer_kernel(
                 reduce_over_k(
                     g,
                     1,
-                    lambda i: [
-                        neg_a[:, g * GROUP + i, :],
-                        log_sigma[:, g * GROUP + i, :],
-                        half_z2[:, i, :],
-                    ],
+                    lambda i: [neg_a[:, g * GROUP + i, :], half_z2[:, i, :]],
                 )
-
-            load_and_quantise(nc, raw_pool, grouped, V_sigma, w_codes, w_scales, alpha_group)
 
             for g in range(N_GROUPS):
                 ds = slice(g * GROUP, (g + 1) * GROUP)
@@ -225,22 +240,22 @@ def tile_rnadeoutputlayer_kernel(
                 for i in range(GROUP):
                     d = g * GROUP + i
                     nc.scalar.activation(
-                        out=log_sigma[:, d, :],
+                        out=sigma_up[:, d, :],
                         in_=acc[:, i, :],
-                        func=ACT.Identity,
-                        bias=bias_sigma[:, d : d + 1],
+                        func=ACT.Relu,
+                        bias=bias_sigma_up[:, d : d + 1],
                         scale=1.0,
                     )
-                nc.vector.tensor_scalar(
-                    out=log_sigma[:, ds, :],
-                    in0=log_sigma[:, ds, :],
-                    scalar1=-20.0,
-                    scalar2=20.0,
-                    op0=ALU.max,
-                    op1=ALU.min,
+                nc.vector.scalar_tensor_tensor(
+                    out=neg_a[:, ds, :],
+                    in0=sigma_up[:, ds, :],
+                    scalar=2.0 * CLIP,
+                    in1=neg_a[:, ds, :],
+                    op0=ALU.min,
+                    op1=ALU.add,
                 )
 
-            load_and_quantise(nc, raw_pool, grouped, V_mu, w_codes, w_scales)
+            load_and_quantise(nc, raw_pool, [grouped], V_mu, w_codes, w_scales)
             for g in range(N_GROUPS):
                 mu_group(g)
 
@@ -264,7 +279,7 @@ def tile_rnadeoutputlayer_kernel(
                 out=result[:],
                 in0=lse_total[:, 1:2],
                 scalar1=lse_total[:, 0:1],
-                scalar2=-D * HALF_LOG_2PI,
+                scalar2=D * (CLIP - HALF_LOG_2PI),
                 op0=ALU.subtract,
                 op1=ALU.add,
             )

@@ -20,16 +20,16 @@ PACK = 4
 HALF = 64
 CHUNK = 8
 RUN = 4
-D_VECTOR = 40
+D_VECTOR_FIRST = 32
+D_VECTOR_LATER = 40
 GROUP = 4
 N_GROUPS = D // GROUP
 HALF_LOG_2PI = 0.5 * math.log(2.0 * math.pi)
-CLIP = 20.0
 
 FLOPS = 2 * ROWS * ROWS * H * D * 3
 
 
-def load_and_quantise(nc, raw_pool, grouped_tiles, src, codes, scales, other_work=None):
+def load_and_quantise(nc, raw_pool, grouped_tiles, d_vector, src, codes, scales, other_work=None):
     by_partition = src.rearrange("r (p j) d -> p r (j d)", j=PACK)
     for half in range(ROWS // HALF):
         grouped = grouped_tiles[half % len(grouped_tiles)]
@@ -40,8 +40,8 @@ def load_and_quantise(nc, raw_pool, grouped_tiles, src, codes, scales, other_wor
             raw_mj = raw[:].rearrange("p r (j d) -> p (r j) d", j=PACK)
             cols = slice(c * CHUNK * PACK, (c + 1) * CHUNK * PACK)
             for copy, d_range in (
-                (nc.vector.tensor_copy, slice(0, D_VECTOR)),
-                (nc.scalar.copy, slice(D_VECTOR, D)),
+                (nc.vector.tensor_copy, slice(0, d_vector)),
+                (nc.scalar.copy, slice(d_vector, D)),
             ):
                 copy(
                     out=grouped[:, d_range, cols].rearrange("p (c i) m -> p c m i", i=RUN),
@@ -80,12 +80,10 @@ def tile_rnadeoutputlayer_kernel(
         nc.scalar.dma_start(out=bias_bf[:, 0, :], in_=b_sigma)
         nc.scalar.dma_start(out=bias_bf[:, 1, :], in_=b_mu)
         nc.scalar.dma_start(out=bias_bf[:, 2, :], in_=b_alpha)
-        bias_sigma_up = keep.tile([P, D], F32)
+        bias_sigma = keep.tile([P, D], F32)
         bias_mu = keep.tile([P, D], F32)
         neg_bias_alpha = keep.tile([P, D], F32)
-        nc.vector.tensor_scalar(
-            out=bias_sigma_up[:], in0=bias_bf[:, 0, :], scalar1=CLIP, scalar2=None, op0=ALU.add
-        )
+        nc.vector.tensor_copy(out=bias_sigma[:], in_=bias_bf[:, 0, :])
         nc.vector.tensor_copy(out=bias_mu[:], in_=bias_bf[:, 1, :])
         nc.vector.tensor_scalar(
             out=neg_bias_alpha[:], in0=bias_bf[:, 2, :], scalar1=-1.0, scalar2=None, op0=ALU.mult
@@ -98,8 +96,6 @@ def tile_rnadeoutputlayer_kernel(
         w_scales = keep.tile([P, D, ROWS], U8, align_bytes=64)
         neg_a = keep.tile([P, D, ROWS], F32)
         y_all = keep.tile([P, D, ROWS], BF16)
-        clip_bias = keep.tile([P, 1], F32)
-        nc.vector.memset(clip_bias[:], CLIP)
         neg_max = keep.tile([P, 2, D], F32)
         exp_sum = keep.tile([P, 2, D], F32)
 
@@ -162,8 +158,10 @@ def tile_rnadeoutputlayer_kernel(
             grouped_too = early.tile([P, D, HALF * PACK], BF16, align_bytes=64)
             two_grouped = [grouped, grouped_too]
 
-            load_and_quantise(nc, raw_pool, two_grouped, x, x_codes, x_scales)
-            load_and_quantise(nc, raw_pool, two_grouped, V_alpha, w_codes, w_scales)
+            load_and_quantise(nc, raw_pool, two_grouped, D_VECTOR_FIRST, x, x_codes, x_scales)
+            load_and_quantise(
+                nc, raw_pool, two_grouped, D_VECTOR_FIRST, V_alpha, w_codes, w_scales
+            )
 
             for g in range(N_GROUPS):
                 acc = products(g)
@@ -190,21 +188,19 @@ def tile_rnadeoutputlayer_kernel(
             def alpha_group(g):
                 reduce_over_k(g, 0, lambda i: [neg_a[:, g * GROUP + i, :]])
 
-            load_and_quantise(nc, raw_pool, two_grouped, V_sigma, w_codes, w_scales, alpha_group)
+            load_and_quantise(
+                nc, raw_pool, two_grouped, D_VECTOR_LATER, V_sigma, w_codes, w_scales, alpha_group
+            )
 
         with tc.tile_pool(name="late", bufs=1) as late:
-            sigma_up = late.tile([P, D, ROWS], F32)
+            log_sigma = late.tile([P, D, ROWS], F32)
 
             def mu_group(g):
                 ds = slice(g * GROUP, (g + 1) * GROUP)
                 acc = products(g)
                 inv_sigma = work.tile([P, GROUP, ROWS], F32, tag="inv_sigma")
                 nc.scalar.activation(
-                    out=inv_sigma[:],
-                    in_=sigma_up[:, ds, :],
-                    func=ACT.Exp,
-                    bias=clip_bias[:],
-                    scale=-1.0,
+                    out=inv_sigma[:], in_=log_sigma[:, ds, :], func=ACT.Exp, scale=-1.0
                 )
                 half_z2 = work.tile([P, GROUP, ROWS], F32, tag="half_z2", bufs=3)
                 for i in range(GROUP):
@@ -217,13 +213,8 @@ def tile_rnadeoutputlayer_kernel(
                         op0=ALU.add,
                         op1=ALU.subtract,
                     )
-                nc.vector.scalar_tensor_tensor(
-                    out=half_z2[:],
-                    in0=inv_sigma[:],
-                    scalar=math.exp(-CLIP),
-                    in1=half_z2[:],
-                    op0=ALU.max,
-                    op1=ALU.mult,
+                nc.vector.tensor_tensor(
+                    out=half_z2[:], in0=half_z2[:], in1=inv_sigma[:], op=ALU.mult
                 )
                 nc.scalar.activation(
                     out=half_z2[:], in_=half_z2[:], func=ACT.Square, scale=math.sqrt(0.5)
@@ -231,7 +222,11 @@ def tile_rnadeoutputlayer_kernel(
                 reduce_over_k(
                     g,
                     1,
-                    lambda i: [neg_a[:, g * GROUP + i, :], half_z2[:, i, :]],
+                    lambda i: [
+                        neg_a[:, g * GROUP + i, :],
+                        log_sigma[:, g * GROUP + i, :],
+                        half_z2[:, i, :],
+                    ],
                 )
 
             for g in range(N_GROUPS):
@@ -240,22 +235,22 @@ def tile_rnadeoutputlayer_kernel(
                 for i in range(GROUP):
                     d = g * GROUP + i
                     nc.scalar.activation(
-                        out=sigma_up[:, d, :],
+                        out=log_sigma[:, d, :],
                         in_=acc[:, i, :],
-                        func=ACT.Relu,
-                        bias=bias_sigma_up[:, d : d + 1],
+                        func=ACT.Identity,
+                        bias=bias_sigma[:, d : d + 1],
                         scale=1.0,
                     )
-                nc.vector.scalar_tensor_tensor(
-                    out=neg_a[:, ds, :],
-                    in0=sigma_up[:, ds, :],
-                    scalar=2.0 * CLIP,
-                    in1=neg_a[:, ds, :],
-                    op0=ALU.min,
-                    op1=ALU.add,
+                nc.vector.tensor_scalar(
+                    out=log_sigma[:, ds, :],
+                    in0=log_sigma[:, ds, :],
+                    scalar1=-20.0,
+                    scalar2=20.0,
+                    op0=ALU.max,
+                    op1=ALU.min,
                 )
 
-            load_and_quantise(nc, raw_pool, [grouped], V_mu, w_codes, w_scales)
+            load_and_quantise(nc, raw_pool, [grouped], D_VECTOR_LATER, V_mu, w_codes, w_scales)
             for g in range(N_GROUPS):
                 mu_group(g)
 
@@ -279,7 +274,7 @@ def tile_rnadeoutputlayer_kernel(
                 out=result[:],
                 in0=lse_total[:, 1:2],
                 scalar1=lse_total[:, 0:1],
-                scalar2=D * (CLIP - HALF_LOG_2PI),
+                scalar2=-D * HALF_LOG_2PI,
                 op0=ALU.subtract,
                 op1=ALU.add,
             )

@@ -24,12 +24,15 @@ D_VECTOR_FIRST = 32
 D_VECTOR_LATER = 40
 GROUP = 4
 N_GROUPS = D // GROUP
+LAG = 2
 HALF_LOG_2PI = 0.5 * math.log(2.0 * math.pi)
 
 FLOPS = 2 * ROWS * ROWS * H * D * 3
 
 
-def load_and_quantise(nc, raw_pool, grouped_tiles, d_vector, src, codes, scales, other_work=None):
+def load_and_quantise(
+    nc, raw_pool, grouped_tiles, d_vector, src, codes, scales, other_work=None, leave_last_half=False
+):
     by_partition = src.rearrange("r (p j) d -> p r (j d)", j=PACK)
     for half in range(ROWS // HALF):
         grouped = grouped_tiles[half % len(grouped_tiles)]
@@ -49,6 +52,8 @@ def load_and_quantise(nc, raw_pool, grouped_tiles, d_vector, src, codes, scales,
                 )
             if other_work is not None:
                 other_work(first_row // CHUNK)
+        if leave_last_half and half == ROWS // HALF - 1:
+            break
         rows = slice(half * HALF, (half + 1) * HALF)
         for d in range(D):
             nc.vector.quantize_mx(
@@ -67,7 +72,8 @@ def tile_rnadeoutputlayer_kernel(
         tc.tile_pool(name="raw", bufs=7) as raw_pool,
         tc.tile_pool(name="work", bufs=2) as work,
         tc.psum_pool(name="acc", bufs=4) as psum_acc,
-        tc.psum_pool(name="tp", bufs=4) as psum_tp,
+        tc.psum_pool(name="tp", bufs=3) as psum_tp,
+        tc.psum_pool(name="spare", bufs=1) as psum_spare,
     ):
         ident = keep.tile([P, P], F32)
         make_identity(nc, ident[:])
@@ -195,9 +201,27 @@ def tile_rnadeoutputlayer_kernel(
         with tc.tile_pool(name="late", bufs=1) as late:
             log_sigma = late.tile([P, D, ROWS], F32)
 
-            def mu_group(g):
+            spare = psum_spare.tile([P, GROUP * ROWS], F32)
+            half_z2_of = {}
+
+            def density(g):
                 ds = slice(g * GROUP, (g + 1) * GROUP)
+                for d in range(g * GROUP, (g + 1) * GROUP):
+                    nc.vector.quantize_mx(
+                        out=w_codes[:, d, HALF:ROWS].bitcast(FP8X4),
+                        scales=w_scales[:, d, HALF:ROWS],
+                        in_=grouped[:, d, :],
+                    )
                 acc = products(g)
+                nc.tensor.matmul_mx(
+                    out=spare[:],
+                    lhsT=x_codes[:, 0, :].bitcast(FP8X4),
+                    lhsT_scale=x_scales[:, 0, :],
+                    rhs=x_codes[:, 0:GROUP, :].rearrange("p d r -> p (d r)").bitcast(FP8X4),
+                    rhs_scale=x_scales[:, 0:GROUP, :].rearrange("p d r -> p (d r)"),
+                    start=True,
+                    stop=True,
+                )
                 inv_sigma = work.tile([P, GROUP, ROWS], F32, tag="inv_sigma")
                 nc.scalar.activation(
                     out=inv_sigma[:], in_=log_sigma[:, ds, :], func=ACT.Exp, scale=-1.0
@@ -219,13 +243,16 @@ def tile_rnadeoutputlayer_kernel(
                 nc.scalar.activation(
                     out=half_z2[:], in_=half_z2[:], func=ACT.Square, scale=math.sqrt(0.5)
                 )
+                half_z2_of[g] = half_z2
+
+            def mixture(g):
                 reduce_over_k(
                     g,
                     1,
                     lambda i: [
                         neg_a[:, g * GROUP + i, :],
                         log_sigma[:, g * GROUP + i, :],
-                        half_z2[:, i, :],
+                        half_z2_of[g][:, i, :],
                     ],
                 )
 
@@ -250,9 +277,15 @@ def tile_rnadeoutputlayer_kernel(
                     op1=ALU.min,
                 )
 
-            load_and_quantise(nc, raw_pool, [grouped], D_VECTOR_LATER, V_mu, w_codes, w_scales)
-            for g in range(N_GROUPS):
-                mu_group(g)
+            load_and_quantise(
+                nc, raw_pool, [grouped], D_VECTOR_LATER, V_mu, w_codes, w_scales, None, True
+            )
+            with tc.manual_schedule(engines={mybir.EngineType.PE}):
+                for g in range(N_GROUPS + LAG):
+                    if g < N_GROUPS:
+                        density(g)
+                    if g >= LAG:
+                        mixture(g - LAG)
 
             log_sum = late.tile([P, 2, D], F32)
             log_total = late.tile([P, 2], F32)

@@ -24,7 +24,8 @@ D_VECTOR_FIRST = 32
 D_VECTOR_LATER = 40
 GROUP = 4
 N_GROUPS = D // GROUP
-LAG = 2
+EVERY_VECTOR = 17
+LAG = 3
 HALF_LOG_2PI = 0.5 * math.log(2.0 * math.pi)
 
 FLOPS = 2 * ROWS * ROWS * H * D * 3
@@ -173,7 +174,7 @@ def tile_rnadeoutputlayer_kernel(
                 acc = products(g)
                 for i in range(GROUP):
                     d = g * GROUP + i
-                    if g % 2 == 0:
+                    if g % EVERY_VECTOR != EVERY_VECTOR - 1:
                         nc.scalar.activation(
                             out=neg_a[:, d, :],
                             in_=acc[:, i, :],
@@ -226,7 +227,7 @@ def tile_rnadeoutputlayer_kernel(
                 nc.scalar.activation(
                     out=inv_sigma[:], in_=log_sigma[:, ds, :], func=ACT.Exp, scale=-1.0
                 )
-                half_z2 = work.tile([P, GROUP, ROWS], F32, tag="half_z2", bufs=3)
+                half_z2 = work.tile([P, GROUP, ROWS], F32, tag="half_z2", bufs=LAG + 1)
                 for i in range(GROUP):
                     d = g * GROUP + i
                     nc.vector.scalar_tensor_tensor(

@@ -24,6 +24,7 @@ D_VECTOR_FIRST = 32
 D_VECTOR_LATER = 40
 GROUP = 4
 N_GROUPS = D // GROUP
+Y_BANK = 8
 EVERY_VECTOR = 17
 LAG = 3
 HALF_LOG_2PI = 0.5 * math.log(2.0 * math.pi)
@@ -148,10 +149,10 @@ def tile_rnadeoutputlayer_kernel(
                     accum_out=exp_sum[:, w, d : d + 1],
                 )
 
-        for g in range(N_GROUPS):
-            spread = psum_acc.tile([P, GROUP, ROWS], F32, tag="acc")
-            for i in range(GROUP):
-                d = g * GROUP + i
+        for first in range(0, D, Y_BANK):
+            spread = psum_acc.tile([P, Y_BANK, ROWS], BF16, tag="acc")
+            for i in range(Y_BANK):
+                d = first + i
                 nc.tensor.matmul(
                     out=spread[:, i, :],
                     lhsT=y_bf[:, d : d + 1].to_broadcast([P, P]),
@@ -159,7 +160,7 @@ def tile_rnadeoutputlayer_kernel(
                     start=True,
                     stop=True,
                 )
-            nc.scalar.copy(out=y_all[:, g * GROUP : (g + 1) * GROUP, :], in_=spread[:])
+            nc.vector.tensor_copy(out=y_all[:, first : first + Y_BANK, :], in_=spread[:])
 
         with tc.tile_pool(name="early", bufs=1) as early:
             grouped_too = early.tile([P, D, HALF * PACK], BF16, align_bytes=64)
@@ -195,8 +196,12 @@ def tile_rnadeoutputlayer_kernel(
             def alpha_group(g):
                 reduce_over_k(g, 0, lambda i: [neg_a[:, g * GROUP + i, :]])
 
+            def alpha_first_half(step):
+                if step % 2 == 0:
+                    alpha_group(step // 2)
+
             load_and_quantise(
-                nc, raw_pool, two_grouped, D_VECTOR_LATER, V_sigma, w_codes, w_scales, alpha_group
+                nc, raw_pool, two_grouped, D_VECTOR_LATER, V_sigma, w_codes, w_scales, alpha_first_half
             )
 
         with tc.tile_pool(name="late", bufs=1) as late:
@@ -278,8 +283,12 @@ def tile_rnadeoutputlayer_kernel(
                     op1=ALU.min,
                 )
 
+            def alpha_second_half(step):
+                if step % 2 == 0:
+                    alpha_group(N_GROUPS // 2 + step // 2)
+
             load_and_quantise(
-                nc, raw_pool, [grouped], D_VECTOR_LATER, V_mu, w_codes, w_scales, None, True
+                nc, raw_pool, [grouped], D_VECTOR_LATER, V_mu, w_codes, w_scales, alpha_second_half, True
             )
             with tc.manual_schedule(engines={mybir.EngineType.PE}):
                 for g in range(N_GROUPS + LAG):

@@ -122,7 +122,7 @@ def tile_rnadeoutputlayer_kernel(
                 )
             return acc
 
-        def reduce_over_k(g, w, terms_of):
+        def turn(terms_of):
             by_b = psum_tp.tile([P, GROUP, ROWS], F32, tag="tp")
             for i in range(GROUP):
                 terms = terms_of(i)
@@ -135,6 +135,9 @@ def tile_rnadeoutputlayer_kernel(
                         start=(t == 0),
                         stop=(t == len(terms) - 1),
                     )
+            return by_b
+
+        def max_and_sum(g, w, by_b):
             ds = slice(g * GROUP, (g + 1) * GROUP)
             nc.vector.tensor_reduce(out=neg_max[:, w, ds], in_=by_b[:], axis=AX.X, op=ALU.min)
             unused = work.tile([P, GROUP, ROWS], BF16, tag="unused")
@@ -148,6 +151,9 @@ def tile_rnadeoutputlayer_kernel(
                     scale=-1.0,
                     accum_out=exp_sum[:, w, d : d + 1],
                 )
+
+        def reduce_over_k(g, w, terms_of):
+            max_and_sum(g, w, turn(terms_of))
 
         for first in range(0, D, Y_BANK):
             spread = psum_acc.tile([P, Y_BANK, ROWS], BF16, tag="acc")
@@ -209,16 +215,22 @@ def tile_rnadeoutputlayer_kernel(
 
             spare = psum_spare.tile([P, GROUP * ROWS], F32)
             half_z2_of = {}
+            inv_sigma_of = {}
 
-            def density(g):
-                ds = slice(g * GROUP, (g + 1) * GROUP)
+            acc_of = {}
+            by_b_of = {}
+
+            def quantise_rest(g):
                 for d in range(g * GROUP, (g + 1) * GROUP):
                     nc.vector.quantize_mx(
                         out=w_codes[:, d, HALF:ROWS].bitcast(FP8X4),
                         scales=w_scales[:, d, HALF:ROWS],
                         in_=grouped[:, d, :],
                     )
-                acc = products(g)
+
+            def passes(g):
+                ds = slice(g * GROUP, (g + 1) * GROUP)
+                acc_of[g] = products(g)
                 nc.tensor.matmul_mx(
                     out=spare[:],
                     lhsT=x_codes[:, 0, :].bitcast(FP8X4),
@@ -232,6 +244,10 @@ def tile_rnadeoutputlayer_kernel(
                 nc.scalar.activation(
                     out=inv_sigma[:], in_=log_sigma[:, ds, :], func=ACT.Exp, scale=-1.0
                 )
+                inv_sigma_of[g] = inv_sigma
+
+            def difference(g):
+                acc = acc_of[g]
                 half_z2 = work.tile([P, GROUP, ROWS], F32, tag="half_z2", bufs=LAG + 1)
                 for i in range(GROUP):
                     d = g * GROUP + i
@@ -243,23 +259,24 @@ def tile_rnadeoutputlayer_kernel(
                         op0=ALU.add,
                         op1=ALU.subtract,
                     )
+                half_z2_of[g] = half_z2
+
+            def scaled_square(g):
+                half_z2 = half_z2_of[g]
                 nc.vector.tensor_tensor(
-                    out=half_z2[:], in0=half_z2[:], in1=inv_sigma[:], op=ALU.mult
+                    out=half_z2[:], in0=half_z2[:], in1=inv_sigma_of[g][:], op=ALU.mult
                 )
                 nc.scalar.activation(
                     out=half_z2[:], in_=half_z2[:], func=ACT.Square, scale=math.sqrt(0.5)
                 )
-                half_z2_of[g] = half_z2
 
-            def mixture(g):
-                reduce_over_k(
-                    g,
-                    1,
+            def exponent(g):
+                by_b_of[g] = turn(
                     lambda i: [
                         neg_a[:, g * GROUP + i, :],
                         log_sigma[:, g * GROUP + i, :],
                         half_z2_of[g][:, i, :],
-                    ],
+                    ]
                 )
 
             for g in range(N_GROUPS):
@@ -290,12 +307,21 @@ def tile_rnadeoutputlayer_kernel(
             load_and_quantise(
                 nc, raw_pool, [grouped], D_VECTOR_LATER, V_mu, w_codes, w_scales, alpha_second_half, True
             )
-            with tc.manual_schedule(engines={mybir.EngineType.PE}):
-                for g in range(N_GROUPS + LAG):
-                    if g < N_GROUPS:
-                        density(g)
-                    if g >= LAG:
-                        mixture(g - LAG)
+            with tc.manual_schedule(engines={mybir.EngineType.PE, mybir.EngineType.DVE}):
+                quantise_rest(0)
+                for s in range(N_GROUPS + LAG + 2):
+                    if s + 1 < N_GROUPS:
+                        quantise_rest(s + 1)
+                    if s < N_GROUPS:
+                        passes(s)
+                    if 1 <= s <= N_GROUPS:
+                        scaled_square(s - 1)
+                    if LAG <= s < N_GROUPS + LAG:
+                        exponent(s - LAG)
+                    if s >= LAG + 1 and s - LAG - 1 < N_GROUPS:
+                        max_and_sum(s - LAG - 1, 1, by_b_of[s - LAG - 1])
+                    if s < N_GROUPS:
+                        difference(s)
 
             log_sum = late.tile([P, 2, D], F32)
             log_total = late.tile([P, 2], F32)

@@ -26,24 +26,30 @@ GROUP = 4
 N_GROUPS = D // GROUP
 Y_BANK = 8
 EVERY_VECTOR = 17
-LAG = 3
+LAG = 2
 HALF_LOG_2PI = 0.5 * math.log(2.0 * math.pi)
 
 FLOPS = 2 * ROWS * ROWS * H * D * 3
 
 
 def load_and_quantise(
-    nc, raw_pool, grouped_tiles, d_vector, src, codes, scales, other_work=None, leave_last_half=False
+    nc, raw_pool, grouped_tiles, d_vector, src, codes, scales, other_work=None, leave_last_half=False,
+    small_start=False,
 ):
     by_partition = src.rearrange("r (p j) d -> p r (j d)", j=PACK)
     for half in range(ROWS // HALF):
         grouped = grouped_tiles[half % len(grouped_tiles)]
-        for c in range(HALF // CHUNK):
-            first_row = half * HALF + c * CHUNK
-            raw = raw_pool.tile([P, CHUNK, PACK * D], BF16)
-            nc.sync.dma_start(out=raw[:], in_=by_partition[:, first_row : first_row + CHUNK, :])
+        sizes = [CHUNK] * (HALF // CHUNK)
+        if small_start and half == 0:
+            sizes = [CHUNK // 4, CHUNK // 4, CHUNK // 2] + sizes[1:]
+        row_in_half = 0
+        for size in sizes:
+            first_row = half * HALF + row_in_half
+            raw = raw_pool.tile([P, size, PACK * D], BF16, tag="raw")
+            nc.sync.dma_start(out=raw[:], in_=by_partition[:, first_row : first_row + size, :])
             raw_mj = raw[:].rearrange("p r (j d) -> p (r j) d", j=PACK)
-            cols = slice(c * CHUNK * PACK, (c + 1) * CHUNK * PACK)
+            cols = slice(row_in_half * PACK, (row_in_half + size) * PACK)
+            row_in_half += size
             for copy, d_range in (
                 (nc.vector.tensor_copy, slice(0, d_vector)),
                 (nc.scalar.copy, slice(d_vector, D)),
@@ -172,7 +178,9 @@ def tile_rnadeoutputlayer_kernel(
             grouped_too = early.tile([P, D, HALF * PACK], BF16, align_bytes=64)
             two_grouped = [grouped, grouped_too]
 
-            load_and_quantise(nc, raw_pool, two_grouped, D_VECTOR_FIRST, x, x_codes, x_scales)
+            load_and_quantise(
+                nc, raw_pool, two_grouped, D_VECTOR_FIRST, x, x_codes, x_scales, None, False, True
+            )
             load_and_quantise(
                 nc, raw_pool, two_grouped, D_VECTOR_FIRST, V_alpha, w_codes, w_scales
             )
@@ -220,6 +228,17 @@ def tile_rnadeoutputlayer_kernel(
             acc_of = {}
             by_b_of = {}
 
+            def extra_pass():
+                nc.tensor.matmul_mx(
+                    out=spare[:],
+                    lhsT=x_codes[:, 0, :].bitcast(FP8X4),
+                    lhsT_scale=x_scales[:, 0, :],
+                    rhs=x_codes[:, 0:GROUP, :].rearrange("p d r -> p (d r)").bitcast(FP8X4),
+                    rhs_scale=x_scales[:, 0:GROUP, :].rearrange("p d r -> p (d r)"),
+                    start=True,
+                    stop=True,
+                )
+
             def quantise_rest(g):
                 for d in range(g * GROUP, (g + 1) * GROUP):
                     nc.vector.quantize_mx(
@@ -231,15 +250,7 @@ def tile_rnadeoutputlayer_kernel(
             def passes(g):
                 ds = slice(g * GROUP, (g + 1) * GROUP)
                 acc_of[g] = products(g)
-                nc.tensor.matmul_mx(
-                    out=spare[:],
-                    lhsT=x_codes[:, 0, :].bitcast(FP8X4),
-                    lhsT_scale=x_scales[:, 0, :],
-                    rhs=x_codes[:, 0:GROUP, :].rearrange("p d r -> p (d r)").bitcast(FP8X4),
-                    rhs_scale=x_scales[:, 0:GROUP, :].rearrange("p d r -> p (d r)"),
-                    start=True,
-                    stop=True,
-                )
+                extra_pass()
                 inv_sigma = work.tile([P, GROUP, ROWS], F32, tag="inv_sigma")
                 nc.scalar.activation(
                     out=inv_sigma[:], in_=log_sigma[:, ds, :], func=ACT.Exp, scale=-1.0
@@ -318,6 +329,9 @@ def tile_rnadeoutputlayer_kernel(
                         scaled_square(s - 1)
                     if LAG <= s < N_GROUPS + LAG:
                         exponent(s - LAG)
+                    if s == N_GROUPS:
+                        extra_pass()
+                        extra_pass()
                     if s >= LAG + 1 and s - LAG - 1 < N_GROUPS:
                         max_and_sum(s - LAG - 1, 1, by_b_of[s - LAG - 1])
                     if s < N_GROUPS:

import math

import concourse.mybir as mybir
from concourse.masks import make_identity

BF16 = mybir.dt.bfloat16
F32 = mybir.dt.float32
U32 = mybir.dt.uint32
U8 = mybir.dt.uint8
FP8X4 = mybir.dt.float8_e4m3fn_x4
ALU = mybir.AluOpType
ACT = mybir.ActivationFunctionType
AX = mybir.AxisListType

P = 128
ROWS = 128
H = 512
D = 64
PACK = 4
HALF = 64
CHUNK = 8
RUN = 4
D_VECTOR_FIRST = 32
D_VECTOR_LATER = 40
GROUP = 4
N_GROUPS = D // GROUP
Y_BANK = 8
EVERY_VECTOR = 17
LAG = 2
HALF_LOG_2PI = 0.5 * math.log(2.0 * math.pi)

FLOPS = 2 * ROWS * ROWS * H * D * 3


def load_and_quantise(
    nc, raw_pool, grouped_tiles, d_vector, src, codes, scales, other_work=None, leave_last_half=False,
    small_start=False,
):
    by_partition = src.rearrange("r (p j) d -> p r (j d)", j=PACK)
    for half in range(ROWS // HALF):
        grouped = grouped_tiles[half % len(grouped_tiles)]
        sizes = [CHUNK] * (HALF // CHUNK)
        if small_start and half == 0:
            sizes = [CHUNK // 4, CHUNK // 4, CHUNK // 2] + sizes[1:]
        row_in_half = 0
        for size in sizes:
            first_row = half * HALF + row_in_half
            raw = raw_pool.tile([P, size, PACK * D], BF16, tag="raw")
            nc.sync.dma_start(out=raw[:], in_=by_partition[:, first_row : first_row + size, :])
            raw_mj = raw[:].rearrange("p r (j d) -> p (r j) d", j=PACK)
            cols = slice(row_in_half * PACK, (row_in_half + size) * PACK)
            row_in_half += size
            for copy, d_range in (
                (nc.vector.tensor_copy, slice(0, d_vector)),
                (nc.scalar.copy, slice(d_vector, D)),
            ):
                copy(
                    out=grouped[:, d_range, cols].rearrange("p (c i) m -> p c m i", i=RUN),
                    in_=raw_mj[:, :, d_range].rearrange("p m (c i) -> p c m i", i=RUN),
                )
            if other_work is not None:
                other_work(first_row // CHUNK)
        if leave_last_half and half == ROWS // HALF - 1:
            break
        rows = slice(half * HALF, (half + 1) * HALF)
        for d in range(D):
            nc.vector.quantize_mx(
                out=codes[:, d, rows].bitcast(FP8X4),
                scales=scales[:, d, rows],
                in_=grouped[:, d, :],
            )


def tile_rnadeoutputlayer_kernel(
    tc, x, input_var, V_alpha, V_mu, V_sigma, b_alpha, b_mu, b_sigma, out
):
    nc = tc.nc
    with (
        tc.tile_pool(name="keep", bufs=1) as keep,
        tc.tile_pool(name="raw", bufs=7) as raw_pool,
        tc.tile_pool(name="work", bufs=2) as work,
        tc.psum_pool(name="acc", bufs=4) as psum_acc,
        tc.psum_pool(name="tp", bufs=3) as psum_tp,
        tc.psum_pool(name="spare", bufs=1) as psum_spare,
    ):
        ident = keep.tile([P, P], F32)
        make_identity(nc, ident[:])
        ident_bf = keep.tile([P, P], BF16)
        make_identity(nc, ident_bf[:])

        y_bf = keep.tile([P, D], BF16)
        nc.scalar.dma_start(out=y_bf[:], in_=input_var)
        bias_bf = keep.tile([P, 3, D], BF16)
        nc.scalar.dma_start(out=bias_bf[:, 0, :], in_=b_sigma)
        nc.scalar.dma_start(out=bias_bf[:, 1, :], in_=b_mu)
        nc.scalar.dma_start(out=bias_bf[:, 2, :], in_=b_alpha)
        bias_sigma = keep.tile([P, D], F32)
        bias_mu = keep.tile([P, D], F32)
        neg_bias_alpha = keep.tile([P, D], F32)
        nc.vector.tensor_copy(out=bias_sigma[:], in_=bias_bf[:, 0, :])
        nc.vector.tensor_copy(out=bias_mu[:], in_=bias_bf[:, 1, :])
        nc.vector.tensor_scalar(
            out=neg_bias_alpha[:], in0=bias_bf[:, 2, :], scalar1=-1.0, scalar2=None, op0=ALU.mult
        )

        grouped = keep.tile([P, D, HALF * PACK], BF16, align_bytes=64)
        x_codes = keep.tile([P, D, ROWS], U32, align_bytes=64)
        x_scales = keep.tile([P, D, ROWS], U8, align_bytes=64)
        w_codes = keep.tile([P, D, ROWS], U32, align_bytes=64)
        w_scales = keep.tile([P, D, ROWS], U8, align_bytes=64)
        neg_a = keep.tile([P, D, ROWS], F32)
        y_all = keep.tile([P, D, ROWS], BF16)
        neg_max = keep.tile([P, 2, D], F32)
        exp_sum = keep.tile([P, 2, D], F32)

        def products(g):
            acc = psum_acc.tile([P, GROUP, ROWS], F32, tag="acc")
            for i in range(GROUP):
                d = g * GROUP + i
                nc.tensor.matmul_mx(
                    out=acc[:, i, :],
                    lhsT=w_codes[:, d, :].bitcast(FP8X4),
                    lhsT_scale=w_scales[:, d, :],
                    rhs=x_codes[:, d, :].bitcast(FP8X4),
                    rhs_scale=x_scales[:, d, :],
                    start=True,
                    stop=True,
                )
            return acc

        def turn(terms_of):
            by_b = psum_tp.tile([P, GROUP, ROWS], F32, tag="tp")
            for i in range(GROUP):
                terms = terms_of(i)
                for t, term in enumerate(terms):
                    nc.tensor.matmul(
                        out=by_b[:, i, :],
                        lhsT=term,
                        rhs=ident[:],
                        is_transpose=True,
                        start=(t == 0),
                        stop=(t == len(terms) - 1),
                    )
            return by_b

        def max_and_sum(g, w, by_b):
            ds = slice(g * GROUP, (g + 1) * GROUP)
            nc.vector.tensor_reduce(out=neg_max[:, w, ds], in_=by_b[:], axis=AX.X, op=ALU.min)
            unused = work.tile([P, GROUP, ROWS], BF16, tag="unused")
            for i in range(GROUP):
                d = g * GROUP + i
                nc.scalar.activation(
                    out=unused[:, i, :],
                    in_=by_b[:, i, :],
                    func=ACT.Exp,
                    bias=neg_max[:, w, d : d + 1],
                    scale=-1.0,
                    accum_out=exp_sum[:, w, d : d + 1],
                )

        def reduce_over_k(g, w, terms_of):
            max_and_sum(g, w, turn(terms_of))

        for first in range(0, D, Y_BANK):
            spread = psum_acc.tile([P, Y_BANK, ROWS], BF16, tag="acc")
            for i in range(Y_BANK):
                d = first + i
                nc.tensor.matmul(
                    out=spread[:, i, :],
                    lhsT=y_bf[:, d : d + 1].to_broadcast([P, P]),
                    rhs=ident_bf[:],
                    start=True,
                    stop=True,
                )
            nc.vector.tensor_copy(out=y_all[:, first : first + Y_BANK, :], in_=spread[:])

        with tc.tile_pool(name="early", bufs=1) as early:
            grouped_too = early.tile([P, D, HALF * PACK], BF16, align_bytes=64)
            two_grouped = [grouped, grouped_too]

            load_and_quantise(
                nc, raw_pool, two_grouped, D_VECTOR_FIRST, x, x_codes, x_scales, None, False, True
            )
            load_and_quantise(
                nc, raw_pool, two_grouped, D_VECTOR_FIRST, V_alpha, w_codes, w_scales
            )

            for g in range(N_GROUPS):
                acc = products(g)
                for i in range(GROUP):
                    d = g * GROUP + i
                    if g % EVERY_VECTOR != EVERY_VECTOR - 1:
                        nc.scalar.activation(
                            out=neg_a[:, d, :],
                            in_=acc[:, i, :],
                            func=ACT.Identity,
                            bias=neg_bias_alpha[:, d : d + 1],
                            scale=-1.0,
                        )
                    else:
                        nc.vector.tensor_scalar(
                            out=neg_a[:, d, :],
                            in0=acc[:, i, :],
                            scalar1=-1.0,
                            scalar2=neg_bias_alpha[:, d : d + 1],
                            op0=ALU.mult,
                            op1=ALU.add,
                        )

            def alpha_group(g):
                reduce_over_k(g, 0, lambda i: [neg_a[:, g * GROUP + i, :]])

            def alpha_first_half(step):
                if step % 2 == 0:
                    alpha_group(step // 2)

            load_and_quantise(
                nc, raw_pool, two_grouped, D_VECTOR_LATER, V_sigma, w_codes, w_scales, alpha_first_half
            )

        with tc.tile_pool(name="late", bufs=1) as late:
            log_sigma = late.tile([P, D, ROWS], F32)

            spare = psum_spare.tile([P, GROUP * ROWS], F32)
            half_z2_of = {}
            inv_sigma_of = {}

            acc_of = {}
            by_b_of = {}

            def extra_pass():
                nc.tensor.matmul_mx(
                    out=spare[:],
                    lhsT=x_codes[:, 0, :].bitcast(FP8X4),
                    lhsT_scale=x_scales[:, 0, :],
                    rhs=x_codes[:, 0:GROUP, :].rearrange("p d r -> p (d r)").bitcast(FP8X4),
                    rhs_scale=x_scales[:, 0:GROUP, :].rearrange("p d r -> p (d r)"),
                    start=True,
                    stop=True,
                )

            def quantise_rest(g):
                for d in range(g * GROUP, (g + 1) * GROUP):
                    nc.vector.quantize_mx(
                        out=w_codes[:, d, HALF:ROWS].bitcast(FP8X4),
                        scales=w_scales[:, d, HALF:ROWS],
                        in_=grouped[:, d, :],
                    )

            def passes(g):
                ds = slice(g * GROUP, (g + 1) * GROUP)
                acc_of[g] = products(g)
                extra_pass()
                inv_sigma = work.tile([P, GROUP, ROWS], F32, tag="inv_sigma")
                nc.scalar.activation(
                    out=inv_sigma[:], in_=log_sigma[:, ds, :], func=ACT.Exp, scale=-1.0
                )
                inv_sigma_of[g] = inv_sigma

            def difference(g):
                acc = acc_of[g]
                half_z2 = work.tile([P, GROUP, ROWS], F32, tag="half_z2", bufs=LAG + 1)
                for i in range(GROUP):
                    d = g * GROUP + i
                    nc.vector.scalar_tensor_tensor(
                        out=half_z2[:, i, :],
                        in0=acc[:, i, :],
                        scalar=bias_mu[:, d : d + 1],
                        in1=y_all[:, d, :],
                        op0=ALU.add,
                        op1=ALU.subtract,
                    )
                half_z2_of[g] = half_z2

            def scaled_square(g):
                half_z2 = half_z2_of[g]
                nc.vector.tensor_tensor(
                    out=half_z2[:], in0=half_z2[:], in1=inv_sigma_of[g][:], op=ALU.mult
                )
                nc.scalar.activation(
                    out=half_z2[:], in_=half_z2[:], func=ACT.Square, scale=math.sqrt(0.5)
                )

            def exponent(g):
                by_b_of[g] = turn(
                    lambda i: [
                        neg_a[:, g * GROUP + i, :],
                        log_sigma[:, g * GROUP + i, :],
                        half_z2_of[g][:, i, :],
                    ]
                )

            for g in range(N_GROUPS):
                ds = slice(g * GROUP, (g + 1) * GROUP)
                acc = products(g)
                for i in range(GROUP):
                    d = g * GROUP + i
                    nc.scalar.activation(
                        out=log_sigma[:, d, :],
                        in_=acc[:, i, :],
                        func=ACT.Identity,
                        bias=bias_sigma[:, d : d + 1],
                        scale=1.0,
                    )
                nc.vector.tensor_scalar(
                    out=log_sigma[:, ds, :],
                    in0=log_sigma[:, ds, :],
                    scalar1=-20.0,
                    scalar2=20.0,
                    op0=ALU.max,
                    op1=ALU.min,
                )

            def alpha_second_half(step):
                if step % 2 == 0:
                    alpha_group(N_GROUPS // 2 + step // 2)

            load_and_quantise(
                nc, raw_pool, [grouped], D_VECTOR_LATER, V_mu, w_codes, w_scales, alpha_second_half, True
            )
            with tc.manual_schedule(engines={mybir.EngineType.PE, mybir.EngineType.DVE}):
                quantise_rest(0)
                for s in range(N_GROUPS + LAG + 2):
                    if s + 1 < N_GROUPS:
                        quantise_rest(s + 1)
                    if s < N_GROUPS:
                        passes(s)
                    if 1 <= s <= N_GROUPS:
                        scaled_square(s - 1)
                    if LAG <= s < N_GROUPS + LAG:
                        exponent(s - LAG)
                    if s == N_GROUPS:
                        extra_pass()
                        extra_pass()
                    if s >= LAG + 1 and s - LAG - 1 < N_GROUPS:
                        max_and_sum(s - LAG - 1, 1, by_b_of[s - LAG - 1])
                    if s < N_GROUPS:
                        difference(s)

            log_sum = late.tile([P, 2, D], F32)
            log_total = late.tile([P, 2], F32)
            for w in range(2):
                nc.scalar.activation(
                    out=log_sum[:, w, :],
                    in_=exp_sum[:, w, :],
                    func=ACT.Ln,
                    accum_out=log_total[:, w : w + 1],
                )
            neg_max_total = late.tile([P, 2], F32)
            nc.vector.tensor_reduce(out=neg_max_total[:], in_=neg_max[:], axis=AX.X, op=ALU.add)
            lse_total = late.tile([P, 2], F32)
            nc.vector.tensor_tensor(
                out=lse_total[:], in0=log_total[:], in1=neg_max_total[:], op=ALU.subtract
            )
            result = late.tile([P, 1], F32)
            nc.vector.tensor_scalar(
                out=result[:],
                in0=lse_total[:, 1:2],
                scalar1=lse_total[:, 0:1],
                scalar2=-D * HALF_LOG_2PI,
                op0=ALU.subtract,
                op1=ALU.add,
            )
            repeated = late.tile([P, P], F32)
            nc.vector.tensor_copy(out=repeated[:], in_=result[:].to_broadcast([P, P]))
            as_row = psum_tp.tile([P, P], F32, tag="tp")
            nc.tensor.transpose(as_row[:], repeated[:], ident[:])
            row = late.tile([P, P], F32)
            nc.vector.tensor_copy(out=row[:], in_=as_row[:])
            nc.sync.dma_start(out=out.rearrange("(o b) -> o b", o=1), in_=row[0:1, :])
